import numpy as np
import ml_dtypes


def mxq(x, axis, fmt="e4m3"):
    dtype, down = {"e4m3": (ml_dtypes.float8_e4m3fn, 7), "e5m2": (ml_dtypes.float8_e5m2, 14)}[fmt]
    v = np.moveaxis(np.asarray(x, np.float32).astype(ml_dtypes.bfloat16).astype(np.float64), axis, -1)
    blocks = v.reshape(v.shape[:-1] + (-1, 32))
    amax = np.abs(blocks).max(-1, keepdims=True)
    byte = np.maximum(np.where(amax > 0, np.frexp(amax)[1] - 1 + 127, 0) - down, 1)
    scale = np.exp2(byte - 127.0)
    codes = (blocks / scale).astype(np.float32).astype(dtype).astype(np.float64)
    return np.moveaxis((codes * scale).reshape(v.shape), -1, axis)


WIDE = False


def mx_kscale(k):
    if not WIDE:
        return np.ones(k)
    levels = np.array([10, -10, 5, -5, 0])
    a = np.random.permutation(np.resize(levels, k // 512 * 4)).reshape(k // 512, 4)
    idx = np.arange(k)
    return np.exp2(a[idx // 512, idx % 128 // 32])


BF16 = ml_dtypes.bfloat16


def bf(x):
    return np.asarray(x, np.float32).astype(BF16)


def f64(x):
    return np.asarray(x).astype(np.float64)


B, L, D, H, P, W = 2, 192, 1024, 4, 128, 128
HD = D // H
LT = L + P


def rotate_half(t):
    h = t.shape[-1] // 2
    return np.concatenate([-t[..., h:], t[..., :h]], axis=-1)


def project(pq, xq, w):
    wm = mxq(f64(w), 0, "e4m3")
    tp = pq @ wm
    tx = xq @ wm
    return np.concatenate([np.broadcast_to(tp, (B, P, D)), tx], axis=1).reshape(B, LT, H, HD)


def setup_inputs():
    s = mx_kscale(D)
    return {"x": bf(np.random.standard_normal((B, L, D)) * s),
            "pmem": bf(np.random.standard_normal((1, P, D)) * s),
            "cos": bf(np.random.uniform(size=(LT, HD))),
            "sin": bf(np.random.uniform(size=(LT, HD))),
            "wq": bf(np.random.standard_normal((D, D)) / np.sqrt(D) / s[:, None]),
            "wk": bf(np.random.standard_normal((D, D)) / np.sqrt(D) / s[:, None]),
            "wv": bf(np.random.standard_normal((D, D)) / np.sqrt(D) / s[:, None])}


def reference(x, pmem, cos, sin, wq, wk, wv):
    pq = mxq(f64(pmem), 2, "e4m3")
    xq = mxq(f64(x), 2, "e4m3")
    q = project(pq, xq, wq)
    k = project(pq, xq, wk)
    v = project(pq, xq, wv)
    cc = f64(cos)[None, :, None, :]
    ss = f64(sin)[None, :, None, :]
    q = q * cc + rotate_half(q) * ss
    k = k * cc + rotate_half(k) * ss
    return q, k, v

@@ -1,0 +1,187 @@
+import concourse.mybir as mybir
+from concourse.masks import make_identity
+
+BF16 = mybir.dt.bfloat16
+F32 = mybir.dt.float32
+U32 = mybir.dt.uint32
+U8 = mybir.dt.uint8
+FP8X4 = mybir.dt.float8_e4m3fn_x4
+ALU = mybir.AluOpType
+
+P = 128
+PACK = 4
+K_PASS = P * PACK
+N_TILE = 512
+
+B, L, D, MEM = 2, 192, 1024, 128
+HD = 256
+HALF = HD // 2
+PASSES = D // K_PASS
+N_BLOCKS = D // N_TILE
+HEADS = N_TILE // HD
+RUN = 4
+
+FLOPS = 2 * (MEM + B * L) * D * 3 * D
+
+EVERY = slice(0, P)
+EVEN = slice(0, P, 2)
+ODD = slice(1, P, 2)
+TILES = 4
+STORE_RUNS = (
+    ((EVERY, 0, 0, P), (EVERY, 1, 0, P)),
+    ((EVERY, 0, MEM, P),),
+    ((EVERY, 1, MEM, P),),
+    ((EVEN, 0, MEM + P, L - P), (ODD, 1, MEM + P, L - P)),
+)
+TABLES = 3
+TABLE_OF_TILE = (0, 1, 1, 2)
+
+
+def load_table(nc, dst, table):
+    nc.sync.dma_start(
+        out=dst[:, 0:2, :], in_=table[0 : 2 * P, :].rearrange("(i p) f -> p i f", p=P)
+    )
+    for partitions in (EVEN, ODD):
+        nc.sync.dma_start(out=dst[partitions, 2, :], in_=table[2 * P :, :])
+
+
+def tile_titanstnt_pa_kernel(tc, x, pmem, cos, sin, wq, wk, wv, out_0, out_1, out_2):
+    nc = tc.nc
+    weights = (wq, wk, wv)
+    outs = (out_0, out_1, out_2)
+    rotated = (True, True, False)
+
+    with (
+        tc.tile_pool(name="keep", bufs=1) as keep,
+        tc.tile_pool(name="stage", bufs=4) as stage,
+        tc.tile_pool(name="prod", bufs=3) as prod,
+        tc.tile_pool(name="result", bufs=6) as result,
+        tc.psum_pool(name="psum", bufs=4) as psum,
+    ):
+        ident = keep.tile([P, P], F32)
+        make_identity(nc, ident[:])
+
+        x_sb = keep.tile([P, TILES, D], BF16)
+        nc.sync.dma_start(out=x_sb[:, 0, :], in_=pmem[0])
+        nc.sync.dma_start(out=x_sb[:, 1:3, :], in_=x[:, 0:P, :].rearrange("b p k -> p b k"))
+        for b, partitions in enumerate((EVEN, ODD)):
+            nc.sync.dma_start(out=x_sb[partitions, 3, :], in_=x[b, P:L, :])
+
+        raw = [[None] * PASSES for m in range(3)]
+
+        def load_weight(m):
+            for g in range(PASSES):
+                raw[m][g] = keep.tile([P, PACK, D], BF16, name="raw%d%d" % (m, g))
+                nc.sync.dma_start(
+                    out=raw[m][g][:],
+                    in_=weights[m][g * K_PASS : (g + 1) * K_PASS, :].rearrange(
+                        "(p j) n -> p j n", j=PACK
+                    ),
+                )
+
+        load_weight(0)
+        factors = keep.tile([P, TABLES, 2, HD], BF16)
+        sin_sb = keep.tile([P, TABLES, HD], BF16)
+        load_table(nc, factors[:, :, 0, :], cos)
+        load_table(nc, sin_sb[:], sin)
+        load_weight(1)
+        load_weight(2)
+
+        x_grouped = keep.tile([P, TILES, PASSES * P * PACK], BF16, align_bytes=64)
+        x_codes = keep.tile([P, TILES, PASSES * P], U32, align_bytes=64)
+        x_scales = keep.tile([P, TILES, PASSES * P], U8, align_bytes=64)
+        for t in range(TILES):
+            words = x_sb[:, t, :].bitcast(F32).rearrange("r (g p u) -> r g u p", g=PASSES, u=2)
+            flipped = psum.tile([P, PASSES, 2, P], F32, tag="plain")
+            for g in range(PASSES):
+                for u in range(2):
+                    nc.tensor.transpose(flipped[:, g, u, :], words[:, g, u, :], ident[:])
+            nc.scalar.copy(
+                out=x_grouped[:, t, :].bitcast(F32).rearrange("p (g r u) -> p g r u", g=PASSES, u=2),
+                in_=flipped[:].rearrange("p g u r -> p g r u"),
+            )
+        for t in range(TILES):
+            nc.vector.quantize_mx(
+                out=x_codes[:, t, :].bitcast(FP8X4), scales=x_scales[:, t, :], in_=x_grouped[:, t, :]
+            )
+
+        w_codes = [keep.tile([P, PASSES, D], U32, align_bytes=64, name="w_codes%d" % m) for m in range(3)]
+        w_scales = [keep.tile([P, PASSES, D], U8, align_bytes=64, name="w_scales%d" % m) for m in range(3)]
+
+        def prepare(m, g, nb):
+            cols = slice(nb * N_TILE, (nb + 1) * N_TILE)
+            grouped = stage.tile([P, N_TILE, PACK], BF16, align_bytes=64)
+            copy = nc.vector.tensor_copy if (m == 0 and nb == 0) else nc.scalar.copy
+            copy(
+                out=grouped[:].rearrange("p (c i) j -> p c j i", i=RUN),
+                in_=raw[m][g][:, :, cols].rearrange("p j (c i) -> p c j i", i=RUN),
+            )
+            nc.vector.quantize_mx(
+                out=w_codes[m][:, g, cols].bitcast(FP8X4),
+                scales=w_scales[m][:, g, cols],
+                in_=grouped[:].rearrange("p n j -> p (n j)"),
+            )
+
+        def project(m, t):
+            rows = result.tile([P, N_BLOCKS, HEADS, 2, HALF], F32)
+            if rotated[m]:
+                products = prod.tile([P, N_BLOCKS, 2, HEADS, 2, HALF], F32)
+            for nb in range(N_BLOCKS):
+                cols = slice(nb * N_TILE, (nb + 1) * N_TILE)
+                acc = psum.tile([P, N_TILE], F32, tag="rot" if rotated[m] else "plain")
+                for g in range(PASSES):
+                    tokens = slice(g * P, (g + 1) * P)
+                    nc.tensor.matmul_mx(
+                        out=acc[:],
+                        lhsT=x_codes[:, t, tokens].bitcast(FP8X4),
+                        lhsT_scale=x_scales[:, t, tokens],
+                        rhs=w_codes[m][:, g, cols].bitcast(FP8X4),
+                        rhs_scale=w_scales[m][:, g, cols],
+                        start=(g == 0),
+                        stop=(g == PASSES - 1),
+                    )
+                if rotated[m]:
+                    shape = [P, 2, HEADS, HD]
+                    nc.vector.tensor_tensor(
+                        out=products[:, nb].rearrange("p c h a f -> p c h (a f)"),
+                        in0=acc[:].rearrange("p (h d) -> p h d", d=HD).unsqueeze(1).to_broadcast(shape),
+                        in1=factors[:, TABLE_OF_TILE[t]].unsqueeze(2).to_broadcast(shape),
+                        op=ALU.mult,
+                    )
+                else:
+                    nc.scalar.copy(out=rows[:, nb].rearrange("p h a f -> p (h a f)"), in_=acc[:])
+            if rotated[m]:
+                nc.gpsimd.tensor_tensor(
+                    out=rows[:, :, :, 0, :],
+                    in0=products[:, :, 0, :, 0, :],
+                    in1=products[:, :, 1, :, 1, :],
+                    op=ALU.subtract,
+                )
+                nc.gpsimd.tensor_tensor(
+                    out=rows[:, :, :, 1, :],
+                    in0=products[:, :, 0, :, 1, :],
+                    in1=products[:, :, 1, :, 0, :],
+                    op=ALU.add,
+                )
+            queue = nc.sync if rotated[m] else nc.scalar
+            for partitions, b, first, count in STORE_RUNS[t]:
+                queue.dma_start(
+                    out=outs[m][b, first : first + count].rearrange("t h d -> t (h d)"),
+                    in_=rows[partitions].rearrange("p n h a f -> p (n h a f)"),
+                )
+
+        for g in range(PASSES):
+            for nb in range(N_BLOCKS):
+                prepare(0, g, nb)
+        for a in range(2):
+            nc.vector.tensor_copy(
+                out=factors[:, :, 1, a * HALF : (a + 1) * HALF],
+                in_=sin_sb[:, :, (1 - a) * HALF : (2 - a) * HALF],
+            )
+        for m in range(3):
+            if m + 1 < 3:
+                for g in range(PASSES):
+                    for nb in range(N_BLOCKS):
+                        prepare(m + 1, g, nb)
+            for t in range(TILES):
+                project(m, t)

@@ -33,155 +33,180 @@ STORE_RUNS = (
     ((EVERY, 1, MEM, P),),
     ((EVEN, 0, MEM + P, L - P), (ODD, 1, MEM + P, L - P)),
 )
-TABLES = 3
-TABLE_OF_TILE = (0, 1, 1, 2)
 
 
-def load_table(nc, dst, table):
-    nc.sync.dma_start(
-        out=dst[:, 0:2, :], in_=table[0 : 2 * P, :].rearrange("(i p) f -> p i f", p=P)
-    )
-    for partitions in (EVEN, ODD):
-        nc.sync.dma_start(out=dst[partitions, 2, :], in_=table[2 * P :, :])
+def load_factors(queue, dst, cos_rows, sin_rows):
+    queue.dma_start(out=dst[..., 0, :], in_=cos_rows)
+    for a in range(2):
+        queue.dma_start(
+            out=dst[..., 1, a * HALF : (a + 1) * HALF],
+            in_=sin_rows[..., (1 - a) * HALF : (2 - a) * HALF],
+        )
 
 
 def tile_titanstnt_pa_kernel(tc, x, pmem, cos, sin, wq, wk, wv, out_0, out_1, out_2):
     nc = tc.nc
     weights = (wq, wk, wv)
     outs = (out_0, out_1, out_2)
-    rotated = (True, True, False)
 
     with (
         tc.tile_pool(name="keep", bufs=1) as keep,
-        tc.tile_pool(name="stage", bufs=4) as stage,
+        tc.tile_pool(name="stage", bufs=8) as stage,
         tc.tile_pool(name="prod", bufs=3) as prod,
-        tc.tile_pool(name="result", bufs=6) as result,
+        tc.tile_pool(name="result", bufs=4) as result,
+        tc.tile_pool(name="plain", bufs=8) as plain,
         tc.psum_pool(name="psum", bufs=4) as psum,
+        tc.manual_schedule(),
     ):
         ident = keep.tile([P, P], F32)
         make_identity(nc, ident[:])
 
-        x_sb = keep.tile([P, TILES, D], BF16)
-        nc.sync.dma_start(out=x_sb[:, 0, :], in_=pmem[0])
-        nc.sync.dma_start(out=x_sb[:, 1:3, :], in_=x[:, 0:P, :].rearrange("b p k -> p b k"))
+        early = keep.tile([P, 2, 2, HD], BF16)
+        late = keep.tile([P, 2, HD], BF16)
+        load_factors(
+            nc.sync,
+            early,
+            cos[0 : 2 * P, :].rearrange("(i p) f -> p i f", p=P),
+            sin[0 : 2 * P, :].rearrange("(i p) f -> p i f", p=P),
+        )
+        for partitions in (EVEN, ODD):
+            load_factors(nc.gpsimd, late[partitions], cos[2 * P :, :], sin[2 * P :, :])
+        factors = (early[:, 0], early[:, 1], early[:, 1], late[:])
+
+        x_first = keep.tile([P, D], BF16)
+        x_middle = keep.tile([P, 2, D], BF16)
+        x_last = keep.tile([P, D], BF16)
+        nc.sync.dma_start(out=x_first[:], in_=pmem[0])
+        nc.sync.dma_start(out=x_middle[:], in_=x[:, 0:P, :].rearrange("b p k -> p b k"))
         for b, partitions in enumerate((EVEN, ODD)):
-            nc.sync.dma_start(out=x_sb[partitions, 3, :], in_=x[b, P:L, :])
+            nc.sync.dma_start(out=x_last[partitions, :], in_=x[b, P:L, :])
+        x_rows = (x_first[:], x_middle[:, 0, :], x_middle[:, 1, :], x_last[:])
 
-        raw = [[None] * PASSES for m in range(3)]
-
-        def load_weight(m):
+        raw = {}
+        for m in range(3):
             for g in range(PASSES):
-                raw[m][g] = keep.tile([P, PACK, D], BF16, name="raw%d%d" % (m, g))
+                raw[m, g] = keep.tile([P, PACK, D], BF16, name="raw%d%d" % (m, g))
                 nc.sync.dma_start(
-                    out=raw[m][g][:],
+                    out=raw[m, g][:],
                     in_=weights[m][g * K_PASS : (g + 1) * K_PASS, :].rearrange(
                         "(p j) n -> p j n", j=PACK
                     ),
                 )
 
-        load_weight(0)
-        factors = keep.tile([P, TABLES, 2, HD], BF16)
-        sin_sb = keep.tile([P, TABLES, HD], BF16)
-        load_table(nc, factors[:, :, 0, :], cos)
-        load_table(nc, sin_sb[:], sin)
-        load_weight(1)
-        load_weight(2)
+        waiting = []
 
-        x_grouped = keep.tile([P, TILES, PASSES * P * PACK], BF16, align_bytes=64)
-        x_codes = keep.tile([P, TILES, PASSES * P], U32, align_bytes=64)
-        x_scales = keep.tile([P, TILES, PASSES * P], U8, align_bytes=64)
-        for t in range(TILES):
-            words = x_sb[:, t, :].bitcast(F32).rearrange("r (g p u) -> r g u p", g=PASSES, u=2)
+        def quantise(n):
+            codes, scales, values = waiting[n]
+            nc.vector.quantize_mx(out=codes[:].bitcast(FP8X4), scales=scales[:], in_=values)
+
+        x_mx = []
+
+        def flip_tokens(t):
+            words = x_rows[t].bitcast(F32).rearrange("r (g p u) -> r g u p", g=PASSES, u=2)
             flipped = psum.tile([P, PASSES, 2, P], F32, tag="plain")
             for g in range(PASSES):
                 for u in range(2):
                     nc.tensor.transpose(flipped[:, g, u, :], words[:, g, u, :], ident[:])
+            grouped = keep.tile([P, PASSES * P * PACK], BF16, align_bytes=64, name="x_grouped%d" % t)
             nc.scalar.copy(
-                out=x_grouped[:, t, :].bitcast(F32).rearrange("p (g r u) -> p g r u", g=PASSES, u=2),
+                out=grouped[:].bitcast(F32).rearrange("p (g r u) -> p g r u", g=PASSES, u=2),
                 in_=flipped[:].rearrange("p g u r -> p g r u"),
             )
-        for t in range(TILES):
-            nc.vector.quantize_mx(
-                out=x_codes[:, t, :].bitcast(FP8X4), scales=x_scales[:, t, :], in_=x_grouped[:, t, :]
-            )
+            codes = keep.tile([P, PASSES * P], U32, align_bytes=64, name="x_codes%d" % t)
+            scales = keep.tile([P, PASSES * P], U8, align_bytes=64, name="x_scales%d" % t)
+            x_mx.append((codes, scales))
+            waiting.append((codes, scales, grouped[:]))
 
-        w_codes = [keep.tile([P, PASSES, D], U32, align_bytes=64, name="w_codes%d" % m) for m in range(3)]
-        w_scales = [keep.tile([P, PASSES, D], U8, align_bytes=64, name="w_scales%d" % m) for m in range(3)]
+        w_mx = {}
 
-        def prepare(m, g, nb):
-            cols = slice(nb * N_TILE, (nb + 1) * N_TILE)
+        def regroup(copy, m, g, nb):
             grouped = stage.tile([P, N_TILE, PACK], BF16, align_bytes=64)
-            copy = nc.vector.tensor_copy if (m == 0 and nb == 0) else nc.scalar.copy
             copy(
                 out=grouped[:].rearrange("p (c i) j -> p c j i", i=RUN),
-                in_=raw[m][g][:, :, cols].rearrange("p j (c i) -> p c j i", i=RUN),
+                in_=raw[m, g][:, :, nb * N_TILE : (nb + 1) * N_TILE].rearrange(
+                    "p j (c i) -> p c j i", i=RUN
+                ),
             )
-            nc.vector.quantize_mx(
-                out=w_codes[m][:, g, cols].bitcast(FP8X4),
-                scales=w_scales[m][:, g, cols],
-                in_=grouped[:].rearrange("p n j -> p (n j)"),
-            )
+            codes = keep.tile([P, N_TILE], U32, align_bytes=64, name="w_codes%d%d%d" % (m, g, nb))
+            scales = keep.tile([P, N_TILE], U8, align_bytes=64, name="w_scales%d%d%d" % (m, g, nb))
+            w_mx[m, g, nb] = (codes, scales)
+            waiting.append((codes, scales, grouped[:].rearrange("p n j -> p (n j)")))
 
-        def project(m, t):
-            rows = result.tile([P, N_BLOCKS, HEADS, 2, HALF], F32)
-            if rotated[m]:
+        def passes(acc, m, t, nb):
+            for g in range(PASSES):
+                tokens = slice(g * P, (g + 1) * P)
+                nc.tensor.matmul_mx(
+                    out=acc[:],
+                    lhsT=x_mx[t][0][:, tokens].bitcast(FP8X4),
+                    lhsT_scale=x_mx[t][1][:, tokens],
+                    rhs=w_mx[m, g, nb][0][:].bitcast(FP8X4),
+                    rhs_scale=w_mx[m, g, nb][1][:],
+                    start=(g == 0),
+                    stop=(g == PASSES - 1),
+                )
+
+        for t in range(TILES):
+            flip_tokens(t)
+            quantise(t)
+        regroup(nc.vector.tensor_copy, 0, 0, 0)
+        regroup(nc.scalar.copy, 0, 0, 1)
+        quantise(TILES)
+        regroup(nc.vector.tensor_copy, 0, 1, 0)
+        regroup(nc.scalar.copy, 0, 1, 1)
+        quantise(TILES + 1)
+        quantise(TILES + 2)
+        done = TILES + 3
+        for m in range(1, 3):
+            for g in range(PASSES):
+                for nb in range(N_BLOCKS):
+                    regroup(nc.scalar.copy, m, g, nb)
+
+        for m in range(2):
+            for t in range(TILES):
+                rows = result.tile([P, N_BLOCKS, HEADS, 2, HALF], F32)
                 products = prod.tile([P, N_BLOCKS, 2, HEADS, 2, HALF], F32)
-            for nb in range(N_BLOCKS):
-                cols = slice(nb * N_TILE, (nb + 1) * N_TILE)
-                acc = psum.tile([P, N_TILE], F32, tag="rot" if rotated[m] else "plain")
-                for g in range(PASSES):
-                    tokens = slice(g * P, (g + 1) * P)
-                    nc.tensor.matmul_mx(
-                        out=acc[:],
-                        lhsT=x_codes[:, t, tokens].bitcast(FP8X4),
-                        lhsT_scale=x_scales[:, t, tokens],
-                        rhs=w_codes[m][:, g, cols].bitcast(FP8X4),
-                        rhs_scale=w_scales[m][:, g, cols],
-                        start=(g == 0),
-                        stop=(g == PASSES - 1),
-                    )
-                if rotated[m]:
+                for nb in range(N_BLOCKS):
+                    bank = (m * TILES + t) * N_BLOCKS + nb
+                    if bank % 3 != 1 and done < len(waiting):
+                        quantise(done)
+                        done += 1
+                    acc = psum.tile([P, N_TILE], F32, tag="rot")
+                    passes(acc, m, t, nb)
                     shape = [P, 2, HEADS, HD]
                     nc.vector.tensor_tensor(
                         out=products[:, nb].rearrange("p c h a f -> p c h (a f)"),
                         in0=acc[:].rearrange("p (h d) -> p h d", d=HD).unsqueeze(1).to_broadcast(shape),
-                        in1=factors[:, TABLE_OF_TILE[t]].unsqueeze(2).to_broadcast(shape),
+                        in1=factors[t].unsqueeze(2).to_broadcast(shape),
                         op=ALU.mult,
                     )
-                else:
-                    nc.scalar.copy(out=rows[:, nb].rearrange("p h a f -> p (h a f)"), in_=acc[:])
-            if rotated[m]:
-                nc.gpsimd.tensor_tensor(
+                adder = nc.vector if (m == 1 and t == TILES - 1) else nc.gpsimd
+                adder.tensor_tensor(
                     out=rows[:, :, :, 0, :],
                     in0=products[:, :, 0, :, 0, :],
                     in1=products[:, :, 1, :, 1, :],
                     op=ALU.subtract,
                 )
-                nc.gpsimd.tensor_tensor(
+                adder.tensor_tensor(
                     out=rows[:, :, :, 1, :],
                     in0=products[:, :, 0, :, 1, :],
                     in1=products[:, :, 1, :, 0, :],
                     op=ALU.add,
                 )
-            queue = nc.sync if rotated[m] else nc.scalar
-            for partitions, b, first, count in STORE_RUNS[t]:
-                queue.dma_start(
-                    out=outs[m][b, first : first + count].rearrange("t h d -> t (h d)"),
-                    in_=rows[partitions].rearrange("p n h a f -> p (n h a f)"),
-                )
+                for partitions, b, first, count in STORE_RUNS[t]:
+                    nc.sync.dma_start(
+                        out=outs[m][b, first : first + count].rearrange("t h d -> t (h d)"),
+                        in_=rows[partitions].rearrange("p n h a f -> p (n h a f)"),
+                    )
 
-        for g in range(PASSES):
-            for nb in range(N_BLOCKS):
-                prepare(0, g, nb)
-        for a in range(2):
-            nc.vector.tensor_copy(
-                out=factors[:, :, 1, a * HALF : (a + 1) * HALF],
-                in_=sin_sb[:, :, (1 - a) * HALF : (2 - a) * HALF],
-            )
-        for m in range(3):
-            if m + 1 < 3:
-                for g in range(PASSES):
-                    for nb in range(N_BLOCKS):
-                        prepare(m + 1, g, nb)
+        for nb in range(N_BLOCKS):
+            cols = slice(nb * N_TILE, (nb + 1) * N_TILE)
             for t in range(TILES):
-                project(m, t)
+                acc = psum.tile([P, N_TILE], F32, tag="plain")
+                passes(acc, 2, t, nb)
+                v_rows = plain.tile([P, N_TILE], F32)
+                nc.scalar.copy(out=v_rows[:], in_=acc[:])
+                for partitions, b, first, count in STORE_RUNS[t]:
+                    nc.scalar.dma_start(
+                        out=outs[2][b, first : first + count].rearrange("t h d -> t (h d)")[:, cols],
+                        in_=v_rows[partitions],
+                    )

@@ -157,10 +157,25 @@ def tile_titanstnt_pa_kernel(tc, x, pmem, cos, sin, wq, wk, wv, out_0, out_1, ou
         quantise(TILES + 2)
         done = TILES + 3
         for m in range(1, 3):
-            for g in range(PASSES):
-                for nb in range(N_BLOCKS):
+            for nb in range(N_BLOCKS):
+                for g in range(PASSES):
                     regroup(nc.scalar.copy, m, g, nb)
 
+        def plain_bank(n):
+            nb, t = divmod(n, TILES)
+            acc = psum.tile([P, N_TILE], F32, tag="plain")
+            passes(acc, 2, t, nb)
+            v_rows = plain.tile([P, N_TILE], F32)
+            nc.scalar.copy(out=v_rows[:], in_=acc[:])
+            for partitions, b, first, count in STORE_RUNS[t]:
+                nc.scalar.dma_start(
+                    out=outs[2][b, first : first + count].rearrange("t h d -> t (h d)")[
+                        :, nb * N_TILE : (nb + 1) * N_TILE
+                    ],
+                    in_=v_rows[partitions],
+                )
+
+        plain_banks = 0
         for m in range(2):
             for t in range(TILES):
                 rows = result.tile([P, N_BLOCKS, HEADS, 2, HALF], F32)
@@ -179,6 +194,11 @@ def tile_titanstnt_pa_kernel(tc, x, pmem, cos, sin, wq, wk, wv, out_0, out_1, ou
                         in1=factors[t].unsqueeze(2).to_broadcast(shape),
                         op=ALU.mult,
                     )
+                    for last_quantise in (9, 12):
+                        if bank > last_quantise and plain_banks < (4 if last_quantise == 9 else 8):
+                            plain_bank(plain_banks)
+                            plain_banks += 1
+                            break
                 adder = nc.vector if (m == 1 and t == TILES - 1) else nc.gpsimd
                 adder.tensor_tensor(
                     out=rows[:, :, :, 0, :],
@@ -198,15 +218,6 @@ def tile_titanstnt_pa_kernel(tc, x, pmem, cos, sin, wq, wk, wv, out_0, out_1, ou
                         in_=rows[partitions].rearrange("p n h a f -> p (n h a f)"),
                     )
 
-        for nb in range(N_BLOCKS):
-            cols = slice(nb * N_TILE, (nb + 1) * N_TILE)
-            for t in range(TILES):
-                acc = psum.tile([P, N_TILE], F32, tag="plain")
-                passes(acc, 2, t, nb)
-                v_rows = plain.tile([P, N_TILE], F32)
-                nc.scalar.copy(out=v_rows[:], in_=acc[:])
-                for partitions, b, first, count in STORE_RUNS[t]:
-                    nc.scalar.dma_start(
-                        out=outs[2][b, first : first + count].rearrange("t h d -> t (h d)")[:, cols],
-                        in_=v_rows[partitions],
-                    )
+        while plain_banks < 2 * TILES:
+            plain_bank(plain_banks)
+            plain_banks += 1

@@ -19,7 +19,7 @@ HALF = HD // 2
 PASSES = D // K_PASS
 N_BLOCKS = D // N_TILE
 HEADS = N_TILE // HD
-RUN = 4
+RUN = 8
 
 FLOPS = 2 * (MEM + B * L) * D * 3 * D
 

@@ -60,18 +60,14 @@ def tile_titanstnt_pa_kernel(tc, x, pmem, cos, sin, wq, wk, wv, out_0, out_1, ou
     ):
         ident = keep.tile([P, P], F32)
         make_identity(nc, ident[:])
+        ident_bf = keep.tile([P, P], BF16)
+        make_identity(nc, ident_bf[:])
 
         early = keep.tile([P, 2, 2, HD], BF16)
         late = keep.tile([P, 2, HD], BF16)
-        load_factors(
-            nc.sync,
-            early,
-            cos[0 : 2 * P, :].rearrange("(i p) f -> p i f", p=P),
-            sin[0 : 2 * P, :].rearrange("(i p) f -> p i f", p=P),
-        )
+        factors = (early[:, 0], early[:, 1], early[:, 1], late[:])
         for partitions in (EVEN, ODD):
             load_factors(nc.gpsimd, late[partitions], cos[2 * P :, :], sin[2 * P :, :])
-        factors = (early[:, 0], early[:, 1], early[:, 1], late[:])
 
         x_first = keep.tile([P, D], BF16)
         x_middle = keep.tile([P, 2, D], BF16)
@@ -92,11 +88,18 @@ def tile_titanstnt_pa_kernel(tc, x, pmem, cos, sin, wq, wk, wv, out_0, out_1, ou
                         "(p j) n -> p j n", j=PACK
                     ),
                 )
+                if (m, g) == (0, 1):
+                    load_factors(
+                        nc.sync,
+                        early,
+                        cos[0 : 2 * P, :].rearrange("(i p) f -> p i f", p=P),
+                        sin[0 : 2 * P, :].rearrange("(i p) f -> p i f", p=P),
+                    )
 
-        waiting = []
+        waiting = {}
 
-        def quantise(n):
-            codes, scales, values = waiting[n]
+        def quantise(*key):
+            codes, scales, values = waiting[key]
             nc.vector.quantize_mx(out=codes[:].bitcast(FP8X4), scales=scales[:], in_=values)
 
         x_mx = []
@@ -115,7 +118,7 @@ def tile_titanstnt_pa_kernel(tc, x, pmem, cos, sin, wq, wk, wv, out_0, out_1, ou
             codes = keep.tile([P, PASSES * P], U32, align_bytes=64, name="x_codes%d" % t)
             scales = keep.tile([P, PASSES * P], U8, align_bytes=64, name="x_scales%d" % t)
             x_mx.append((codes, scales))
-            waiting.append((codes, scales, grouped[:]))
+            waiting[t,] = (codes, scales, grouped[:])
 
         w_mx = {}
 
@@ -130,7 +133,26 @@ def tile_titanstnt_pa_kernel(tc, x, pmem, cos, sin, wq, wk, wv, out_0, out_1, ou
             codes = keep.tile([P, N_TILE], U32, align_bytes=64, name="w_codes%d%d%d" % (m, g, nb))
             scales = keep.tile([P, N_TILE], U8, align_bytes=64, name="w_scales%d%d%d" % (m, g, nb))
             w_mx[m, g, nb] = (codes, scales)
-            waiting.append((codes, scales, grouped[:].rearrange("p n j -> p (n j)")))
+            waiting[m, g, nb] = (codes, scales, grouped[:].rearrange("p n j -> p (n j)"))
+
+        def regroup_by_tensor(copy, m, g, nb):
+            grouped = stage.tile([P, N_TILE, PACK], BF16, align_bytes=64, tag="grouped")
+            for c in range(2):
+                woven = psum.tile([P, N_TILE // 2, PACK], BF16, tag="plain")
+                for h in range(2):
+                    first = nb * N_TILE + (2 * c + h) * P
+                    nc.tensor.matmul(
+                        woven[:, h * P : (h + 1) * P, :].rearrange("p n j -> p (n j)"),
+                        lhsT=ident_bf[:],
+                        rhs=raw[m, g][:, :, first : first + P].rearrange("p j n -> p n j"),
+                        start=True,
+                        stop=True,
+                    )
+                copy(out=grouped[:, 2 * c * P : (2 * c + 2) * P], in_=woven[:])
+            codes = keep.tile([P, N_TILE], U32, align_bytes=64, name="w_codes%d%d%d" % (m, g, nb))
+            scales = keep.tile([P, N_TILE], U8, align_bytes=64, name="w_scales%d%d%d" % (m, g, nb))
+            w_mx[m, g, nb] = (codes, scales)
+            waiting[m, g, nb] = (codes, scales, grouped[:].rearrange("p n j -> p (n j)"))
 
         def passes(acc, m, t, nb):
             for g in range(PASSES):
@@ -145,24 +167,7 @@ def tile_titanstnt_pa_kernel(tc, x, pmem, cos, sin, wq, wk, wv, out_0, out_1, ou
                     stop=(g == PASSES - 1),
                 )
 
-        for t in range(TILES):
-            flip_tokens(t)
-            quantise(t)
-        regroup(nc.vector.tensor_copy, 0, 0, 0)
-        regroup(nc.scalar.copy, 0, 0, 1)
-        quantise(TILES)
-        regroup(nc.vector.tensor_copy, 0, 1, 0)
-        regroup(nc.scalar.copy, 0, 1, 1)
-        quantise(TILES + 1)
-        quantise(TILES + 2)
-        done = TILES + 3
-        for m in range(1, 3):
-            for nb in range(N_BLOCKS):
-                for g in range(PASSES):
-                    regroup(nc.scalar.copy, m, g, nb)
-
-        def plain_bank(n):
-            nb, t = divmod(n, TILES)
+        def plain_bank(nb, t):
             acc = psum.tile([P, N_TILE], F32, tag="plain")
             passes(acc, 2, t, nb)
             v_rows = plain.tile([P, N_TILE], F32)
@@ -175,49 +180,121 @@ def tile_titanstnt_pa_kernel(tc, x, pmem, cos, sin, wq, wk, wv, out_0, out_1, ou
                     in_=v_rows[partitions],
                 )
 
-        plain_banks = 0
-        for m in range(2):
-            for t in range(TILES):
-                rows = result.tile([P, N_BLOCKS, HEADS, 2, HALF], F32)
-                products = prod.tile([P, N_BLOCKS, 2, HEADS, 2, HALF], F32)
-                for nb in range(N_BLOCKS):
-                    bank = (m * TILES + t) * N_BLOCKS + nb
-                    if bank % 3 != 1 and done < len(waiting):
-                        quantise(done)
-                        done += 1
-                    acc = psum.tile([P, N_TILE], F32, tag="rot")
-                    passes(acc, m, t, nb)
-                    shape = [P, 2, HEADS, HD]
-                    nc.vector.tensor_tensor(
-                        out=products[:, nb].rearrange("p c h a f -> p c h (a f)"),
-                        in0=acc[:].rearrange("p (h d) -> p h d", d=HD).unsqueeze(1).to_broadcast(shape),
-                        in1=factors[t].unsqueeze(2).to_broadcast(shape),
-                        op=ALU.mult,
-                    )
-                    for last_quantise in (9, 12):
-                        if bank > last_quantise and plain_banks < (4 if last_quantise == 9 else 8):
-                            plain_bank(plain_banks)
-                            plain_banks += 1
-                            break
-                adder = nc.vector if (m == 1 and t == TILES - 1) else nc.gpsimd
-                adder.tensor_tensor(
-                    out=rows[:, :, :, 0, :],
-                    in0=products[:, :, 0, :, 0, :],
-                    in1=products[:, :, 1, :, 1, :],
-                    op=ALU.subtract,
-                )
-                adder.tensor_tensor(
-                    out=rows[:, :, :, 1, :],
-                    in0=products[:, :, 0, :, 1, :],
-                    in1=products[:, :, 1, :, 0, :],
-                    op=ALU.add,
-                )
-                for partitions, b, first, count in STORE_RUNS[t]:
-                    nc.sync.dma_start(
-                        out=outs[m][b, first : first + count].rearrange("t h d -> t (h d)"),
-                        in_=rows[partitions].rearrange("p n h a f -> p (n h a f)"),
-                    )
+        products = {}
 
-        while plain_banks < 2 * TILES:
-            plain_bank(plain_banks)
-            plain_banks += 1
+        def rotate(m, t, nb):
+            if (m, t) not in products:
+                products[m, t] = prod.tile([P, N_BLOCKS, 2, HEADS, 2, HALF], F32, name="products")
+            acc = psum.tile([P, N_TILE], F32, tag="rot")
+            passes(acc, m, t, nb)
+            shape = [P, 2, HEADS, HD]
+            nc.vector.tensor_tensor(
+                out=products[m, t][:, nb].rearrange("p c h a f -> p c h (a f)"),
+                in0=acc[:].rearrange("p (h d) -> p h d", d=HD).unsqueeze(1).to_broadcast(shape),
+                in1=factors[t].unsqueeze(2).to_broadcast(shape),
+                op=ALU.mult,
+            )
+
+        def add_and_store(adder, m, t):
+            both = products[m, t]
+            rows = result.tile([P, N_BLOCKS, HEADS, 2, HALF], F32)
+            adder.tensor_tensor(
+                out=rows[:, :, :, 0, :],
+                in0=both[:, :, 0, :, 0, :],
+                in1=both[:, :, 1, :, 1, :],
+                op=ALU.subtract,
+            )
+            adder.tensor_tensor(
+                out=rows[:, :, :, 1, :],
+                in0=both[:, :, 0, :, 1, :],
+                in1=both[:, :, 1, :, 0, :],
+                op=ALU.add,
+            )
+            for partitions, b, first, count in STORE_RUNS[t]:
+                nc.sync.dma_start(
+                    out=outs[m][b, first : first + count].rearrange("t h d -> t (h d)"),
+                    in_=rows[partitions].rearrange("p n h a f -> p (n h a f)"),
+                )
+
+        def add_bank_and_store(adder, m, t, nb):
+            both = products[m, t][:, nb]
+            rows = result.tile([P, HEADS, 2, HALF], F32, tag="half_rows")
+            adder.tensor_tensor(
+                out=rows[:, :, 0, :], in0=both[:, 0, :, 0, :], in1=both[:, 1, :, 1, :], op=ALU.subtract
+            )
+            adder.tensor_tensor(
+                out=rows[:, :, 1, :], in0=both[:, 0, :, 1, :], in1=both[:, 1, :, 0, :], op=ALU.add
+            )
+            for partitions, b, first, count in STORE_RUNS[t]:
+                nc.sync.dma_start(
+                    out=outs[m][b, first : first + count].rearrange("t h d -> t (h d)")[
+                        :, nb * N_TILE : (nb + 1) * N_TILE
+                    ],
+                    in_=rows[partitions].rearrange("p h a f -> p (h a f)"),
+                )
+
+        G, V = nc.gpsimd, nc.vector
+        flip_tokens(0)
+        quantise(0)
+        flip_tokens(1)
+        quantise(1)
+        flip_tokens(2)
+        quantise(2)
+        flip_tokens(3)
+        regroup(nc.vector.tensor_copy, 0, 0, 0)
+        quantise(3)
+        regroup(nc.scalar.copy, 0, 0, 1)
+        quantise(0, 0, 0)
+        regroup(nc.vector.tensor_copy, 0, 1, 0)
+        quantise(0, 0, 1)
+        quantise(0, 1, 0)
+        regroup(nc.scalar.copy, 0, 1, 1)
+        regroup(nc.scalar.copy, 1, 0, 0)
+        regroup(nc.scalar.copy, 1, 1, 0)
+        regroup(nc.scalar.copy, 1, 0, 1)
+        regroup(nc.scalar.copy, 1, 1, 1)
+        regroup(nc.scalar.copy, 2, 0, 0)
+        regroup(nc.scalar.copy, 2, 1, 0)
+        quantise(0, 1, 1)
+        rotate(0, 0, 0)
+        rotate(0, 0, 1)
+        add_and_store(G, 0, 0)
+        rotate(0, 1, 0)
+        quantise(1, 0, 0)
+        rotate(0, 1, 1)
+        add_and_store(G, 0, 1)
+        quantise(1, 1, 0)
+        rotate(0, 2, 0)
+        quantise(1, 0, 1)
+        rotate(0, 2, 1)
+        add_and_store(G, 0, 2)
+        quantise(1, 1, 1)
+        rotate(0, 3, 0)
+        regroup_by_tensor(nc.scalar.copy, 2, 0, 1)
+        rotate(0, 3, 1)
+        add_and_store(G, 0, 3)
+        rotate(1, 0, 0)
+        regroup_by_tensor(nc.scalar.copy, 2, 1, 1)
+        quantise(2, 0, 0)
+        rotate(1, 0, 1)
+        add_and_store(G, 1, 0)
+        quantise(2, 1, 0)
+        rotate(1, 1, 0)
+        quantise(2, 0, 1)
+        rotate(1, 1, 1)
+        add_and_store(G, 1, 1)
+        quantise(2, 1, 1)
+        rotate(1, 2, 0)
+        plain_bank(0, 0)
+        plain_bank(0, 1)
+        rotate(1, 2, 1)
+        plain_bank(0, 2)
+        plain_bank(0, 3)
+        add_and_store(G, 1, 2)
+        rotate(1, 3, 0)
+        plain_bank(1, 0)
+        plain_bank(1, 1)
+        rotate(1, 3, 1)
+        add_and_store(V, 1, 3)
+        plain_bank(1, 2)
+        plain_bank(1, 3)

@@ -142,9 +142,9 @@ def tile_titanstnt_pa_kernel(tc, x, pmem, cos, sin, wq, wk, wv, out_0, out_1, ou
                 for h in range(2):
                     first = nb * N_TILE + (2 * c + h) * P
                     nc.tensor.matmul(
-                        woven[:, h * P : (h + 1) * P, :].rearrange("p n j -> p (n j)"),
+                        woven[:, h * P : (h + 1) * P, :].rearrange("p n j -> p j n"),
                         lhsT=ident_bf[:],
-                        rhs=raw[m, g][:, :, first : first + P].rearrange("p j n -> p n j"),
+                        rhs=raw[m, g][:, :, first : first + P],
                         start=True,
                         stop=True,
                     )

@@ -271,30 +271,30 @@ def tile_titanstnt_pa_kernel(tc, x, pmem, cos, sin, wq, wk, wv, out_0, out_1, ou
         quantise(1, 1, 1)
         rotate(0, 3, 0)
         regroup_by_tensor(nc.scalar.copy, 2, 0, 1)
+        quantise(2, 0, 0)
         rotate(0, 3, 1)
         add_and_store(G, 0, 3)
-        rotate(1, 0, 0)
         regroup_by_tensor(nc.scalar.copy, 2, 1, 1)
-        quantise(2, 0, 0)
+        quantise(2, 1, 0)
+        rotate(1, 0, 0)
+        quantise(2, 0, 1)
         rotate(1, 0, 1)
         add_and_store(G, 1, 0)
-        quantise(2, 1, 0)
-        rotate(1, 1, 0)
-        quantise(2, 0, 1)
-        rotate(1, 1, 1)
-        add_and_store(G, 1, 1)
         quantise(2, 1, 1)
-        rotate(1, 2, 0)
+        rotate(1, 1, 0)
         plain_bank(0, 0)
         plain_bank(0, 1)
-        rotate(1, 2, 1)
+        rotate(1, 1, 1)
+        add_and_store(G, 1, 1)
         plain_bank(0, 2)
         plain_bank(0, 3)
-        add_and_store(G, 1, 2)
-        rotate(1, 3, 0)
+        rotate(1, 2, 0)
         plain_bank(1, 0)
         plain_bank(1, 1)
-        rotate(1, 3, 1)
-        add_and_store(V, 1, 3)
+        rotate(1, 2, 1)
+        add_and_store(G, 1, 2)
         plain_bank(1, 2)
         plain_bank(1, 3)
+        rotate(1, 3, 0)
+        rotate(1, 3, 1)
+        add_and_store(V, 1, 3)

@@ -122,37 +122,41 @@ def tile_titanstnt_pa_kernel(tc, x, pmem, cos, sin, wq, wk, wv, out_0, out_1, ou
 
         w_mx = {}
 
-        def regroup(copy, m, g, nb):
+        grouped_of = {}
+
+        def stage_chunk(m, g, nb):
             grouped = stage.tile([P, N_TILE, PACK], BF16, align_bytes=64)
-            copy(
-                out=grouped[:].rearrange("p (c i) j -> p c j i", i=RUN),
-                in_=raw[m, g][:, :, nb * N_TILE : (nb + 1) * N_TILE].rearrange(
-                    "p j (c i) -> p c j i", i=RUN
-                ),
-            )
             codes = keep.tile([P, N_TILE], U32, align_bytes=64, name="w_codes%d%d%d" % (m, g, nb))
             scales = keep.tile([P, N_TILE], U8, align_bytes=64, name="w_scales%d%d%d" % (m, g, nb))
+            grouped_of[m, g, nb] = grouped
             w_mx[m, g, nb] = (codes, scales)
             waiting[m, g, nb] = (codes, scales, grouped[:].rearrange("p n j -> p (n j)"))
 
-        def regroup_by_tensor(copy, m, g, nb):
-            grouped = stage.tile([P, N_TILE, PACK], BF16, align_bytes=64, tag="grouped")
-            for c in range(2):
-                woven = psum.tile([P, N_TILE // 2, PACK], BF16, tag="plain")
-                for h in range(2):
-                    first = nb * N_TILE + (2 * c + h) * P
-                    nc.tensor.matmul(
-                        woven[:, h * P : (h + 1) * P, :].rearrange("p n j -> p j n"),
-                        lhsT=ident_bf[:],
-                        rhs=raw[m, g][:, :, first : first + P],
-                        start=True,
-                        stop=True,
-                    )
-                copy(out=grouped[:, 2 * c * P : (2 * c + 2) * P], in_=woven[:])
-            codes = keep.tile([P, N_TILE], U32, align_bytes=64, name="w_codes%d%d%d" % (m, g, nb))
-            scales = keep.tile([P, N_TILE], U8, align_bytes=64, name="w_scales%d%d%d" % (m, g, nb))
-            w_mx[m, g, nb] = (codes, scales)
-            waiting[m, g, nb] = (codes, scales, grouped[:].rearrange("p n j -> p (n j)"))
+        def regroup(copy, m, g, nb, columns=N_TILE):
+            stage_chunk(m, g, nb)
+            copy(
+                out=grouped_of[m, g, nb][:, 0:columns].rearrange("p (c i) j -> p c j i", i=RUN),
+                in_=raw[m, g][:, :, nb * N_TILE : nb * N_TILE + columns].rearrange(
+                    "p j (c i) -> p c j i", i=RUN
+                ),
+            )
+
+        def weave(m, g, nb, c):
+            if (m, g, nb) not in grouped_of:
+                stage_chunk(m, g, nb)
+            woven = psum.tile([P, N_TILE // 2, PACK], BF16, tag="plain")
+            for h in range(2):
+                first = nb * N_TILE + (2 * c + h) * P
+                nc.tensor.matmul(
+                    woven[:, h * P : (h + 1) * P, :].rearrange("p n j -> p j n"),
+                    lhsT=ident_bf[:],
+                    rhs=raw[m, g][:, :, first : first + P],
+                    start=True,
+                    stop=True,
+                )
+            nc.scalar.copy(
+                out=grouped_of[m, g, nb][:, 2 * c * P : (2 * c + 2) * P], in_=woven[:]
+            )
 
         def passes(acc, m, t, nb):
             for g in range(PASSES):
@@ -216,23 +220,6 @@ def tile_titanstnt_pa_kernel(tc, x, pmem, cos, sin, wq, wk, wv, out_0, out_1, ou
                     in_=rows[partitions].rearrange("p n h a f -> p (n h a f)"),
                 )
 
-        def add_bank_and_store(adder, m, t, nb):
-            both = products[m, t][:, nb]
-            rows = result.tile([P, HEADS, 2, HALF], F32, tag="half_rows")
-            adder.tensor_tensor(
-                out=rows[:, :, 0, :], in0=both[:, 0, :, 0, :], in1=both[:, 1, :, 1, :], op=ALU.subtract
-            )
-            adder.tensor_tensor(
-                out=rows[:, :, 1, :], in0=both[:, 0, :, 1, :], in1=both[:, 1, :, 0, :], op=ALU.add
-            )
-            for partitions, b, first, count in STORE_RUNS[t]:
-                nc.sync.dma_start(
-                    out=outs[m][b, first : first + count].rearrange("t h d -> t (h d)")[
-                        :, nb * N_TILE : (nb + 1) * N_TILE
-                    ],
-                    in_=rows[partitions].rearrange("p h a f -> p (h a f)"),
-                )
-
         G, V = nc.gpsimd, nc.vector
         flip_tokens(0)
         quantise(0)
@@ -248,52 +235,56 @@ def tile_titanstnt_pa_kernel(tc, x, pmem, cos, sin, wq, wk, wv, out_0, out_1, ou
         regroup(nc.vector.tensor_copy, 0, 1, 0)
         quantise(0, 0, 1)
         quantise(0, 1, 0)
-        regroup(nc.scalar.copy, 0, 1, 1)
+        regroup(nc.scalar.copy, 0, 1, 1, columns=N_TILE // 2)
+        weave(0, 1, 1, 1)
         regroup(nc.scalar.copy, 1, 0, 0)
         regroup(nc.scalar.copy, 1, 1, 0)
-        regroup(nc.scalar.copy, 1, 0, 1)
-        regroup(nc.scalar.copy, 1, 1, 1)
-        regroup(nc.scalar.copy, 2, 0, 0)
-        regroup(nc.scalar.copy, 2, 1, 0)
         quantise(0, 1, 1)
         rotate(0, 0, 0)
         rotate(0, 0, 1)
         add_and_store(G, 0, 0)
         rotate(0, 1, 0)
+        weave(1, 0, 1, 0)
         quantise(1, 0, 0)
         rotate(0, 1, 1)
+        weave(1, 0, 1, 1)
         add_and_store(G, 0, 1)
         quantise(1, 1, 0)
         rotate(0, 2, 0)
+        regroup(nc.scalar.copy, 1, 1, 1)
         quantise(1, 0, 1)
         rotate(0, 2, 1)
         add_and_store(G, 0, 2)
+        regroup(nc.scalar.copy, 2, 0, 0)
+        regroup(nc.scalar.copy, 2, 1, 0)
         quantise(1, 1, 1)
         rotate(0, 3, 0)
-        regroup_by_tensor(nc.scalar.copy, 2, 0, 1)
+        weave(2, 0, 1, 0)
         quantise(2, 0, 0)
         rotate(0, 3, 1)
+        weave(2, 0, 1, 1)
         add_and_store(G, 0, 3)
-        regroup_by_tensor(nc.scalar.copy, 2, 1, 1)
         quantise(2, 1, 0)
         rotate(1, 0, 0)
+        weave(2, 1, 1, 0)
         quantise(2, 0, 1)
         rotate(1, 0, 1)
+        weave(2, 1, 1, 1)
         add_and_store(G, 1, 0)
-        quantise(2, 1, 1)
-        rotate(1, 1, 0)
         plain_bank(0, 0)
         plain_bank(0, 1)
-        rotate(1, 1, 1)
-        add_and_store(G, 1, 1)
+        quantise(2, 1, 1)
+        rotate(1, 1, 0)
         plain_bank(0, 2)
         plain_bank(0, 3)
+        rotate(1, 1, 1)
+        add_and_store(G, 1, 1)
         rotate(1, 2, 0)
         plain_bank(1, 0)
         plain_bank(1, 1)
         rotate(1, 2, 1)
-        add_and_store(G, 1, 2)
         plain_bank(1, 2)
+        add_and_store(G, 1, 2)
         plain_bank(1, 3)
         rotate(1, 3, 0)
         rotate(1, 3, 1)

@@ -251,7 +251,8 @@ def tile_titanstnt_pa_kernel(tc, x, pmem, cos, sin, wq, wk, wv, out_0, out_1, ou
         add_and_store(G, 0, 1)
         quantise(1, 1, 0)
         rotate(0, 2, 0)
-        regroup(nc.scalar.copy, 1, 1, 1)
+        regroup(nc.scalar.copy, 1, 1, 1, columns=N_TILE // 2)
+        weave(1, 1, 1, 1)
         quantise(1, 0, 1)
         rotate(0, 2, 1)
         add_and_store(G, 0, 2)

import concourse.mybir as mybir
from concourse.masks import make_identity

BF16 = mybir.dt.bfloat16
F32 = mybir.dt.float32
U32 = mybir.dt.uint32
U8 = mybir.dt.uint8
FP8X4 = mybir.dt.float8_e4m3fn_x4
ALU = mybir.AluOpType

P = 128
PACK = 4
K_PASS = P * PACK
N_TILE = 512

B, L, D, MEM = 2, 192, 1024, 128
HD = 256
HALF = HD // 2
PASSES = D // K_PASS
N_BLOCKS = D // N_TILE
HEADS = N_TILE // HD
RUN = 8

FLOPS = 2 * (MEM + B * L) * D * 3 * D

EVERY = slice(0, P)
EVEN = slice(0, P, 2)
ODD = slice(1, P, 2)
TILES = 4
STORE_RUNS = (
    ((EVERY, 0, 0, P), (EVERY, 1, 0, P)),
    ((EVERY, 0, MEM, P),),
    ((EVERY, 1, MEM, P),),
    ((EVEN, 0, MEM + P, L - P), (ODD, 1, MEM + P, L - P)),
)


def load_factors(queue, dst, cos_rows, sin_rows):
    queue.dma_start(out=dst[..., 0, :], in_=cos_rows)
    for a in range(2):
        queue.dma_start(
            out=dst[..., 1, a * HALF : (a + 1) * HALF],
            in_=sin_rows[..., (1 - a) * HALF : (2 - a) * HALF],
        )


def tile_titanstnt_pa_kernel(tc, x, pmem, cos, sin, wq, wk, wv, out_0, out_1, out_2):
    nc = tc.nc
    weights = (wq, wk, wv)
    outs = (out_0, out_1, out_2)

    with (
        tc.tile_pool(name="keep", bufs=1) as keep,
        tc.tile_pool(name="stage", bufs=8) as stage,
        tc.tile_pool(name="prod", bufs=3) as prod,
        tc.tile_pool(name="result", bufs=4) as result,
        tc.tile_pool(name="plain", bufs=8) as plain,
        tc.psum_pool(name="psum", bufs=4) as psum,
        tc.manual_schedule(),
    ):
        ident = keep.tile([P, P], F32)
        make_identity(nc, ident[:])
        ident_bf = keep.tile([P, P], BF16)
        make_identity(nc, ident_bf[:])

        early = keep.tile([P, 2, 2, HD], BF16)
        late = keep.tile([P, 2, HD], BF16)
        factors = (early[:, 0], early[:, 1], early[:, 1], late[:])
        for partitions in (EVEN, ODD):
            load_factors(nc.gpsimd, late[partitions], cos[2 * P :, :], sin[2 * P :, :])

        x_first = keep.tile([P, D], BF16)
        x_middle = keep.tile([P, 2, D], BF16)
        x_last = keep.tile([P, D], BF16)
        nc.sync.dma_start(out=x_first[:], in_=pmem[0])
        nc.sync.dma_start(out=x_middle[:], in_=x[:, 0:P, :].rearrange("b p k -> p b k"))
        for b, partitions in enumerate((EVEN, ODD)):
            nc.sync.dma_start(out=x_last[partitions, :], in_=x[b, P:L, :])
        x_rows = (x_first[:], x_middle[:, 0, :], x_middle[:, 1, :], x_last[:])

        raw = {}
        for m in range(3):
            for g in range(PASSES):
                raw[m, g] = keep.tile([P, PACK, D], BF16, name="raw%d%d" % (m, g))
                nc.sync.dma_start(
                    out=raw[m, g][:],
                    in_=weights[m][g * K_PASS : (g + 1) * K_PASS, :].rearrange(
                        "(p j) n -> p j n", j=PACK
                    ),
                )
                if (m, g) == (0, 1):
                    load_factors(
                        nc.sync,
                        early,
                        cos[0 : 2 * P, :].rearrange("(i p) f -> p i f", p=P),
                        sin[0 : 2 * P, :].rearrange("(i p) f -> p i f", p=P),
                    )

        waiting = {}

        def quantise(*key):
            codes, scales, values = waiting[key]
            nc.vector.quantize_mx(out=codes[:].bitcast(FP8X4), scales=scales[:], in_=values)

        x_mx = []

        def flip_tokens(t):
            words = x_rows[t].bitcast(F32).rearrange("r (g p u) -> r g u p", g=PASSES, u=2)
            flipped = psum.tile([P, PASSES, 2, P], F32, tag="plain")
            for g in range(PASSES):
                for u in range(2):
                    nc.tensor.transpose(flipped[:, g, u, :], words[:, g, u, :], ident[:])
            grouped = keep.tile([P, PASSES * P * PACK], BF16, align_bytes=64, name="x_grouped%d" % t)
            nc.scalar.copy(
                out=grouped[:].bitcast(F32).rearrange("p (g r u) -> p g r u", g=PASSES, u=2),
                in_=flipped[:].rearrange("p g u r -> p g r u"),
            )
            codes = keep.tile([P, PASSES * P], U32, align_bytes=64, name="x_codes%d" % t)
            scales = keep.tile([P, PASSES * P], U8, align_bytes=64, name="x_scales%d" % t)
            x_mx.append((codes, scales))
            waiting[t,] = (codes, scales, grouped[:])

        w_mx = {}

        grouped_of = {}

        def stage_chunk(m, g, nb):
            grouped = stage.tile([P, N_TILE, PACK], BF16, align_bytes=64)
            codes = keep.tile([P, N_TILE], U32, align_bytes=64, name="w_codes%d%d%d" % (m, g, nb))
            scales = keep.tile([P, N_TILE], U8, align_bytes=64, name="w_scales%d%d%d" % (m, g, nb))
            grouped_of[m, g, nb] = grouped
            w_mx[m, g, nb] = (codes, scales)
            waiting[m, g, nb] = (codes, scales, grouped[:].rearrange("p n j -> p (n j)"))

        def regroup(copy, m, g, nb, columns=N_TILE):
            stage_chunk(m, g, nb)
            copy(
                out=grouped_of[m, g, nb][:, 0:columns].rearrange("p (c i) j -> p c j i", i=RUN),
                in_=raw[m, g][:, :, nb * N_TILE : nb * N_TILE + columns].rearrange(
                    "p j (c i) -> p c j i", i=RUN
                ),
            )

        def weave(m, g, nb, c):
            if (m, g, nb) not in grouped_of:
                stage_chunk(m, g, nb)
            woven = psum.tile([P, N_TILE // 2, PACK], BF16, tag="plain")
            for h in range(2):
                first = nb * N_TILE + (2 * c + h) * P
                nc.tensor.matmul(
                    woven[:, h * P : (h + 1) * P, :].rearrange("p n j -> p j n"),
                    lhsT=ident_bf[:],
                    rhs=raw[m, g][:, :, first : first + P],
                    start=True,
                    stop=True,
                )
            nc.scalar.copy(
                out=grouped_of[m, g, nb][:, 2 * c * P : (2 * c + 2) * P], in_=woven[:]
            )

        def passes(acc, m, t, nb):
            for g in range(PASSES):
                tokens = slice(g * P, (g + 1) * P)
                nc.tensor.matmul_mx(
                    out=acc[:],
                    lhsT=x_mx[t][0][:, tokens].bitcast(FP8X4),
                    lhsT_scale=x_mx[t][1][:, tokens],
                    rhs=w_mx[m, g, nb][0][:].bitcast(FP8X4),
                    rhs_scale=w_mx[m, g, nb][1][:],
                    start=(g == 0),
                    stop=(g == PASSES - 1),
                )

        def plain_bank(nb, t):
            acc = psum.tile([P, N_TILE], F32, tag="plain")
            passes(acc, 2, t, nb)
            v_rows = plain.tile([P, N_TILE], F32)
            nc.scalar.copy(out=v_rows[:], in_=acc[:])
            for partitions, b, first, count in STORE_RUNS[t]:
                nc.scalar.dma_start(
                    out=outs[2][b, first : first + count].rearrange("t h d -> t (h d)")[
                        :, nb * N_TILE : (nb + 1) * N_TILE
                    ],
                    in_=v_rows[partitions],
                )

        products = {}

        def rotate(m, t, nb):
            if (m, t) not in products:
                products[m, t] = prod.tile([P, N_BLOCKS, 2, HEADS, 2, HALF], F32, name="products")
            acc = psum.tile([P, N_TILE], F32, tag="rot")
            passes(acc, m, t, nb)
            shape = [P, 2, HEADS, HD]
            nc.vector.tensor_tensor(
                out=products[m, t][:, nb].rearrange("p c h a f -> p c h (a f)"),
                in0=acc[:].rearrange("p (h d) -> p h d", d=HD).unsqueeze(1).to_broadcast(shape),
                in1=factors[t].unsqueeze(2).to_broadcast(shape),
                op=ALU.mult,
            )

        def add_and_store(adder, m, t):
            both = products[m, t]
            rows = result.tile([P, N_BLOCKS, HEADS, 2, HALF], F32)
            adder.tensor_tensor(
                out=rows[:, :, :, 0, :],
                in0=both[:, :, 0, :, 0, :],
                in1=both[:, :, 1, :, 1, :],
                op=ALU.subtract,
            )
            adder.tensor_tensor(
                out=rows[:, :, :, 1, :],
                in0=both[:, :, 0, :, 1, :],
                in1=both[:, :, 1, :, 0, :],
                op=ALU.add,
            )
            for partitions, b, first, count in STORE_RUNS[t]:
                nc.sync.dma_start(
                    out=outs[m][b, first : first + count].rearrange("t h d -> t (h d)"),
                    in_=rows[partitions].rearrange("p n h a f -> p (n h a f)"),
                )

        G, V = nc.gpsimd, nc.vector
        flip_tokens(0)
        quantise(0)
        flip_tokens(1)
        quantise(1)
        flip_tokens(2)
        quantise(2)
        flip_tokens(3)
        regroup(nc.vector.tensor_copy, 0, 0, 0)
        quantise(3)
        regroup(nc.scalar.copy, 0, 0, 1)
        quantise(0, 0, 0)
        regroup(nc.vector.tensor_copy, 0, 1, 0)
        quantise(0, 0, 1)
        quantise(0, 1, 0)
        regroup(nc.scalar.copy, 0, 1, 1, columns=N_TILE // 2)
        weave(0, 1, 1, 1)
        regroup(nc.scalar.copy, 1, 0, 0)
        regroup(nc.scalar.copy, 1, 1, 0)
        quantise(0, 1, 1)
        rotate(0, 0, 0)
        rotate(0, 0, 1)
        add_and_store(G, 0, 0)
        rotate(0, 1, 0)
        weave(1, 0, 1, 0)
        quantise(1, 0, 0)
        rotate(0, 1, 1)
        weave(1, 0, 1, 1)
        add_and_store(G, 0, 1)
        quantise(1, 1, 0)
        rotate(0, 2, 0)
        regroup(nc.scalar.copy, 1, 1, 1, columns=N_TILE // 2)
        weave(1, 1, 1, 1)
        quantise(1, 0, 1)
        rotate(0, 2, 1)
        add_and_store(G, 0, 2)
        regroup(nc.scalar.copy, 2, 0, 0)
        regroup(nc.scalar.copy, 2, 1, 0)
        quantise(1, 1, 1)
        rotate(0, 3, 0)
        weave(2, 0, 1, 0)
        quantise(2, 0, 0)
        rotate(0, 3, 1)
        weave(2, 0, 1, 1)
        add_and_store(G, 0, 3)
        quantise(2, 1, 0)
        rotate(1, 0, 0)
        weave(2, 1, 1, 0)
        quantise(2, 0, 1)
        rotate(1, 0, 1)
        weave(2, 1, 1, 1)
        add_and_store(G, 1, 0)
        plain_bank(0, 0)
        plain_bank(0, 1)
        quantise(2, 1, 1)
        rotate(1, 1, 0)
        plain_bank(0, 2)
        plain_bank(0, 3)
        rotate(1, 1, 1)
        add_and_store(G, 1, 1)
        rotate(1, 2, 0)
        plain_bank(1, 0)
        plain_bank(1, 1)
        rotate(1, 2, 1)
        plain_bank(1, 2)
        add_and_store(G, 1, 2)
        plain_bank(1, 3)
        rotate(1, 3, 0)
        rotate(1, 3, 1)
        add_and_store(V, 1, 3)
